import numpy as np
import ml_dtypes


def mxq(x, axis, fmt="e4m3"):
    dtype, down = {"e4m3": (ml_dtypes.float8_e4m3fn, 7), "e5m2": (ml_dtypes.float8_e5m2, 14)}[fmt]
    v = np.moveaxis(np.asarray(x, np.float32).astype(ml_dtypes.bfloat16).astype(np.float64), axis, -1)
    blocks = v.reshape(v.shape[:-1] + (-1, 32))
    amax = np.abs(blocks).max(-1, keepdims=True)
    byte = np.maximum(np.where(amax > 0, np.frexp(amax)[1] - 1 + 127, 0) - down, 1)
    scale = np.exp2(byte - 127.0)
    codes = (blocks / scale).astype(np.float32).astype(dtype).astype(np.float64)
    return np.moveaxis((codes * scale).reshape(v.shape), -1, axis)


WIDE = False


def mx_kscale(k):
    if not WIDE:
        return np.ones(k)
    levels = np.array([10, -10, 5, -5, 0])
    a = np.random.permutation(np.resize(levels, k // 512 * 4)).reshape(k // 512, 4)
    idx = np.arange(k)
    return np.exp2(a[idx // 512, idx % 128 // 32])


BF16 = ml_dtypes.bfloat16


def bf(x):
    return np.asarray(x, np.float32).astype(BF16)


def f64(x):
    return np.asarray(x).astype(np.float64)


E2M1 = np.array([0.0, 0.5, 1.0, 1.5, 2.0, 3.0, 4.0, 6.0, -0.0, -0.5, -1.0, -1.5, -2.0, -3.0, -4.0, -6.0])


def pack_weight(w, fmt):
    k, n = w.shape
    w = f64(bf(w)).reshape(k // 32, 32, n)
    amax = np.abs(w).max(1)
    if fmt == "e4m3":
        byte = np.frexp(amax)[1] - 1 + 127 - 7
    else:
        mant, ex = np.frexp(amax / 6.0)
        byte = np.where(mant > 0.5, ex, ex - 1) + 127
    byte = np.clip(np.where(amax > 0, byte, 1), 1, 254)
    scaled = (w * np.exp2(127.0 - byte)[:, None, :]).reshape(k, n).astype(np.float32)
    by_word = np.ascontiguousarray(scaled.reshape(k // 512, 128, 4, n).transpose(0, 1, 3, 2))
    if fmt == "e4m3":
        words = by_word.astype(ml_dtypes.float8_e4m3fn).view(np.uint8)
    else:
        c = by_word.astype(ml_dtypes.float4_e2m1fn).view(np.uint8) & 0xF
        words = c[..., 0::2] | (c[..., 1::2] << 4)
    return np.ascontiguousarray(words), np.ascontiguousarray(byte.astype(np.uint8).reshape(k // 512, 16, n))


def unpack_weight(words, scales, fmt):
    g, p, n, _ = words.shape
    if fmt == "e4m3":
        vals = np.ascontiguousarray(words).view(ml_dtypes.float8_e4m3fn).astype(np.float64)
    else:
        nib = np.empty((g, p, n, 4), np.uint8)
        nib[..., 0::2] = words & 0xF
        nib[..., 1::2] = words >> 4
        vals = E2M1[nib]
    vals = vals * np.repeat(np.exp2(scales.astype(np.float64) - 127.0), 8, axis=1)[..., None]
    return vals.transpose(0, 1, 3, 2).reshape(g * 512, n)


BS, N, D, B, D_PM = 2, 1024, 1024, 8, 512


def sigmoid(v):
    return 1.0 / (1.0 + np.exp(-v))


def setup_inputs():
    k = mx_kscale(D)
    m = 3.0 * np.random.rand(BS, N, 1)
    H = bf(np.random.standard_normal((BS, N, D)) * k)
    surprise = bf(np.random.standard_normal((BS, N, D)) * m)
    w = np.random.standard_normal((D_PM, D)) / np.sqrt(D) / k
    words, scales = pack_weight(np.ascontiguousarray(w.T), "e4m3")
    return {"H": H,
            "surprise": surprise,
            "proj_in_w_words": words,
            "proj_in_w_scales": scales,
            "proj_in_b": bf(np.random.standard_normal(D_PM) * 0.1),
            "surp_scale": bf((1.0 + 0.1 * np.random.standard_normal(1)) / np.sqrt(D)),
            "surp_bias": bf(-1.5 + 0.1 * np.random.standard_normal(1))}


def reference(H, surprise, proj_in_w_words, proj_in_w_scales, proj_in_b, surp_scale, surp_bias):
    pre = (mxq(f64(H), 2, "e4m3") @ unpack_weight(proj_in_w_words, proj_in_w_scales, "e4m3")) + f64(proj_in_b)
    surp_mag = np.sqrt(np.sum(f64(surprise) ** 2, axis=-1))
    s = sigmoid(f64(surp_scale) * surp_mag + f64(surp_bias))
    weighted = np.sqrt(s)[..., None] * pre
    wq = mxq(weighted, 1, "e4m3")
    return (wq.transpose(0, 2, 1) @ wq) / N

@@ -1,0 +1,227 @@
+import concourse.mybir as mybir
+from concourse.masks import make_identity
+
+F32 = mybir.dt.float32
+BF16 = mybir.dt.bfloat16
+I32 = mybir.dt.int32
+U32 = mybir.dt.uint32
+U8 = mybir.dt.uint8
+FP8X4 = mybir.dt.float8_e4m3fn_x4
+ALU = mybir.AluOpType
+ACT = mybir.ActivationFunctionType
+
+P = 128
+PACK = 4
+K_PASS = P * PACK
+SAMPLES, TOKENS, D, D_PM = 2, 1024, 1024, 512
+CHUNKS = SAMPLES * TOKENS // K_PASS
+CHUNKS_PER_SAMPLE = TOKENS // K_PASS
+K_GROUPS = D // K_PASS
+HALF = 2
+HALVES = PACK // HALF
+M_TILES = D_PM // P
+UNITS = CHUNKS * HALVES
+VECTOR_COPY_UNITS = 2
+
+FLOPS = 2 * SAMPLES * TOKENS * D * D_PM + 2 * SAMPLES * D_PM * D_PM * TOKENS
+
+
+def tile_proceduralmemory_pa_kernel(
+    tc, H, surprise, proj_in_w_words, proj_in_w_scales, proj_in_b, surp_scale, surp_bias, out
+):
+    nc = tc.nc
+    h_dram = H.flatten_outer_dims().rearrange("(c p t) k -> c p t k", p=P, t=PACK)
+    s_dram = surprise.flatten_outer_dims().rearrange("(c p t) k -> c p t k", p=P, t=PACK)
+
+    with tc.tile_pool(name="const", bufs=1) as const, tc.tile_pool(name="inputs", bufs=UNITS) as inputs, tc.tile_pool(
+        name="work", bufs=3
+    ) as work, tc.tile_pool(name="chunkwork", bufs=2) as chunkwork, tc.tile_pool(
+        name="outputs", bufs=M_TILES
+    ) as outputs, tc.psum_pool(name="xt_psum", bufs=HALF) as xt_psum, tc.psum_pool(
+        name="pre_psum", bufs=HALF
+    ) as pre_psum, tc.psum_pool(name="g_psum", bufs=M_TILES) as g_psum, tc.manual_schedule():
+        w_scales = const.tile([P, K_GROUPS, D_PM], U8, align_bytes=64)
+        nc.vector.memset(w_scales[:].bitcast(I32), 0)
+        w_codes = const.tile([P, K_GROUPS, D_PM], U32, align_bytes=64)
+
+        one_column = const.tile([P, 1], F32)
+        nc.vector.memset(one_column[:], 0.0)
+        nc.scalar.activation(out=one_column[:], in_=one_column[:], func=ACT.Sigmoid)
+
+        ident = const.tile([P, P], F32)
+        make_identity(nc, ident[:])
+        half_power = const.tile([P, PACK], F32)
+        nc.gpsimd.memset(half_power[:], 0.5)
+
+        bias_bf = const.tile([P, D_PM], BF16)
+        nc.gpsimd.dma_start(out=bias_bf[:], in_=proj_in_b.partition_broadcast(P))
+        gain_bf = const.tile([P, 1], BF16)
+        nc.gpsimd.dma_start(out=gain_bf[:], in_=surp_scale.partition_broadcast(P))
+        shift_bf = const.tile([P, 1], BF16)
+        nc.gpsimd.dma_start(out=shift_bf[:], in_=surp_bias.partition_broadcast(P))
+        gain = const.tile([P, 1], F32)
+        nc.gpsimd.tensor_copy(out=gain[:], in_=gain_bf[:])
+        shift = const.tile([P, 1], F32)
+        nc.gpsimd.tensor_copy(out=shift[:], in_=shift_bf[:])
+
+        sum_sq = const.tile([P, CHUNKS, PACK], F32)
+        mag = const.tile([P, CHUNKS, PACK], F32)
+        sig = const.tile([P, CHUNKS, PACK], F32)
+        gate = const.tile([P, CHUNKS, PACK], F32)
+
+        wq_codes = const.tile([P, CHUNKS, D_PM], U32, align_bytes=64)
+        wq_scales = const.tile([P, CHUNKS, D_PM], U8, align_bytes=64)
+
+        s_sb, h_sb = [], []
+        for u in range(UNITS):
+            tiles = slice((u % HALVES) * HALF, (u % HALVES + 1) * HALF)
+            s_half = inputs.tile([P, HALF, D], BF16, name="s_half")
+            nc.sync.dma_start(out=s_half[:], in_=s_dram[u // HALVES][:, tiles, :])
+            s_sb.append(s_half)
+            h_half = inputs.tile([P, HALF, D], BF16, name="h_half")
+            nc.sync.dma_start(out=h_half[:], in_=h_dram[u // HALVES][:, tiles, :])
+            h_sb.append(h_half)
+            if u == 0:
+                nc.sync.dma_start(
+                    out=w_codes[:].bitcast(I32),
+                    in_=proj_in_w_words.rearrange("g p n t -> p g (n t)").bitcast(I32),
+                )
+                scale_rows = proj_in_w_scales.rearrange("g (q r) n -> q r g n", r=PACK)
+                for quadrant in range(PACK):
+                    nc.sync.dma_start(
+                        out=w_scales[32 * quadrant : 32 * quadrant + PACK, :, :].bitcast(I32),
+                        in_=scale_rows[quadrant].bitcast(I32),
+                    )
+
+        h_grouped, h_codes, h_scales, acc, pre, w_grouped, g_acc = {}, {}, {}, {}, {}, {}, {}
+
+        def sums_of_squares(u):
+            for j in range(HALF):
+                t = (u % HALVES) * HALF + j
+                squares = work.tile([P, D], BF16, name="squares")
+                nc.scalar.activation(
+                    out=squares[:], in_=s_sb[u][:, j, :], func=ACT.Square,
+                    accum_out=sum_sq[:, u // HALVES, t : t + 1],
+                )
+
+        def transpose_h(u):
+            h_grouped[u] = work.tile([P, HALF, K_GROUPS * P * PACK], BF16, align_bytes=64, name="h_grouped")
+            for j in range(HALF):
+                h_words = h_sb[u][:, j, :].bitcast(F32)
+                xt = xt_psum.tile([P, K_GROUPS, 2, P], F32, name="xt")
+                for g in range(K_GROUPS):
+                    for w in range(2):
+                        first = g * (K_PASS // 2) + w
+                        nc.tensor.transpose(
+                            xt[:, g, w, :], h_words[:, first : (g + 1) * (K_PASS // 2) : 2], ident[:]
+                        )
+                grouped_words = h_grouped[u][:, j, :].bitcast(F32).rearrange("p (g n w) -> p g n w", g=K_GROUPS, w=2)
+                if u < VECTOR_COPY_UNITS:
+                    nc.vector.tensor_copy(out=grouped_words, in_=xt[:].rearrange("p g w n -> p g n w"))
+                else:
+                    nc.scalar.copy(out=grouped_words, in_=xt[:].rearrange("p g w n -> p g n w"))
+
+        def quantise_h(u):
+            h_codes[u] = work.tile([P, HALF, K_GROUPS, P], U32, align_bytes=64, name="h_codes")
+            h_scales[u] = work.tile([P, HALF, K_GROUPS, P], U8, align_bytes=64, name="h_scales")
+            nc.vector.quantize_mx(
+                out=h_codes[u][:].rearrange("p j g n -> p (j g n)").bitcast(FP8X4),
+                scales=h_scales[u][:].rearrange("p j g n -> p (j g n)"),
+                in_=h_grouped[u][:].rearrange("p j x -> p (j x)"),
+            )
+
+        def project(u):
+            for j in range(HALF):
+                acc[u, j] = pre_psum.tile([P, D_PM], F32, name="acc")
+                for g in range(K_GROUPS):
+                    nc.tensor.matmul_mx(
+                        out=acc[u, j][:],
+                        lhsT=h_codes[u][:, j, g, :].bitcast(FP8X4),
+                        lhsT_scale=h_scales[u][:, j, g, :],
+                        rhs=w_codes[:, g, :].bitcast(FP8X4),
+                        rhs_scale=w_scales[:, g, :],
+                        start=(g == 0),
+                        stop=(g == K_GROUPS - 1),
+                    )
+
+        def add_bias(u):
+            c = u // HALVES
+            if u % HALVES == 0:
+                pre[c] = chunkwork.tile([P, PACK, D_PM], F32, name="pre")
+            for j in range(HALF):
+                t = (u % HALVES) * HALF + j
+                nc.vector.tensor_tensor(out=pre[c][:, t, :], in0=acc[u, j][:], in1=bias_bf[:], op=ALU.add)
+
+        def magnitude(c):
+            nc.gpsimd.tensor_tensor(out=mag[:, c, :], in0=sum_sq[:, c, :], in1=half_power[:], op=ALU.pow)
+
+        def gate_of(c):
+            nc.scalar.activation(
+                out=sig[:, c, :], in_=mag[:, c, :], func=ACT.Sigmoid, scale=gain[:, 0:1], bias=shift[:, 0:1]
+            )
+            nc.gpsimd.tensor_tensor(out=gate[:, c, :], in0=sig[:, c, :], in1=half_power[:], op=ALU.pow)
+
+        def weigh(c):
+            w_grouped[c] = chunkwork.tile([P, D_PM, PACK], BF16, align_bytes=64, name="w_grouped")
+            nc.vector.tensor_tensor(
+                out=w_grouped[c][:],
+                in0=pre[c][:].rearrange("p t n -> p n t"),
+                in1=gate[:, c, :].unsqueeze(1).to_broadcast([P, D_PM, PACK]),
+                op=ALU.mult,
+            )
+
+        def quantise_weighted(c):
+            nc.vector.quantize_mx(
+                out=wq_codes[:, c, :].bitcast(FP8X4),
+                scales=wq_scales[:, c, :],
+                in_=w_grouped[c][:].rearrange("p n t -> p (n t)"),
+            )
+
+        def gram_pass(c):
+            b, q = c // CHUNKS_PER_SAMPLE, c % CHUNKS_PER_SAMPLE
+            for m in range(M_TILES):
+                rows = slice(m * P, (m + 1) * P)
+                if q == 0:
+                    g_acc[b, m] = g_psum.tile([P, D_PM], F32, name="g_acc")
+                nc.tensor.matmul_mx(
+                    out=g_acc[b, m][:],
+                    lhsT=wq_codes[:, c, rows].bitcast(FP8X4),
+                    lhsT_scale=wq_scales[:, c, rows],
+                    rhs=wq_codes[:, c, :].bitcast(FP8X4),
+                    rhs_scale=wq_scales[:, c, :],
+                    start=(q == 0),
+                    stop=(q == CHUNKS_PER_SAMPLE - 1),
+                )
+
+        def store_gram(b):
+            for m in range(M_TILES):
+                g_sb = outputs.tile([P, D_PM], F32, name="g_sb")
+                if b == SAMPLES - 1 and m % 2 == 1:
+                    nc.vector.tensor_scalar_mul(out=g_sb[:], in0=g_acc[b, m][:], scalar1=1.0 / TOKENS)
+                else:
+                    nc.scalar.mul(out=g_sb[:], in_=g_acc[b, m][:], mul=1.0 / TOKENS)
+                nc.sync.dma_start(out=out[b, m * P : (m + 1) * P, :], in_=g_sb[:])
+
+        for s in range(UNITS + 3):
+            if s < UNITS:
+                sums_of_squares(s)
+                if s % HALVES == HALVES - 1:
+                    magnitude(s // HALVES)
+            if HALVES <= s <= UNITS and s % HALVES == 0:
+                gate_of(s // HALVES - 1)
+            if s == UNITS:
+                store_gram(0)
+            if 0 <= s - 1 < UNITS:
+                quantise_h(s - 1)
+            if s < UNITS:
+                transpose_h(s)
+            if 0 <= s - 1 < UNITS:
+                project(s - 1)
+            if s >= 4 and s % HALVES == 0:
+                quantise_weighted((s - 4) // HALVES)
+                gram_pass((s - 4) // HALVES)
+            if 0 <= s - 2 < UNITS:
+                add_bias(s - 2)
+            if s >= 3 and s % HALVES == 1:
+                weigh((s - 3) // HALVES)
+        store_gram(1)

@@ -133,7 +133,7 @@ def tile_proceduralmemory_pa_kernel(
         def project(u):
             for j in range(HALF):
                 acc[u, j] = pre_psum.tile([P, D_PM], F32, name="acc")
-                for g in range(K_GROUPS):
+                for g in [0, 1, 0, 1]:
                     nc.tensor.matmul_mx(
                         out=acc[u, j][:],
                         lhsT=h_codes[u][:, j, g, :].bitcast(FP8X4),

@@ -133,7 +133,7 @@ def tile_proceduralmemory_pa_kernel(
         def project(u):
             for j in range(HALF):
                 acc[u, j] = pre_psum.tile([P, D_PM], F32, name="acc")
-                for g in [0, 1, 0, 1]:
+                for g in range(K_GROUPS):
                     nc.tensor.matmul_mx(
                         out=acc[u, j][:],
                         lhsT=h_codes[u][:, j, g, :].bitcast(FP8X4),
@@ -162,12 +162,13 @@ def tile_proceduralmemory_pa_kernel(
             nc.gpsimd.tensor_tensor(out=gate[:, c, :], in0=sig[:, c, :], in1=half_power[:], op=ALU.pow)
 
         def weigh(c):
+            weighted = chunkwork.tile([P, PACK, D_PM], BF16, name="weighted")
+            for t in range(PACK):
+                nc.vector.tensor_scalar_mul(out=weighted[:, t, :], in0=pre[c][:, t, :], scalar1=gate[:, c, t : t + 1])
             w_grouped[c] = chunkwork.tile([P, D_PM, PACK], BF16, align_bytes=64, name="w_grouped")
-            nc.vector.tensor_tensor(
-                out=w_grouped[c][:],
-                in0=pre[c][:].rearrange("p t n -> p n t"),
-                in1=gate[:, c, :].unsqueeze(1).to_broadcast([P, D_PM, PACK]),
-                op=ALU.mult,
+            nc.vector.tensor_copy(
+                out=w_grouped[c][:].rearrange("p (n i) t -> p n t i", i=4),
+                in_=weighted[:].rearrange("p t (n i) -> p n t i", i=4),
             )
 
         def quantise_weighted(c):

@@ -21,6 +21,7 @@ HALF = 2
 HALVES = PACK // HALF
 M_TILES = D_PM // P
 UNITS = CHUNKS * HALVES
+SMALL_STEP = 16
 VECTOR_COPY_UNITS = 2
 
 FLOPS = 2 * SAMPLES * TOKENS * D * D_PM + 2 * SAMPLES * D_PM * D_PM * TOKENS
@@ -53,16 +54,25 @@ def tile_proceduralmemory_pa_kernel(
         half_power = const.tile([P, PACK], F32)
         nc.gpsimd.memset(half_power[:], 0.5)
 
-        bias_bf = const.tile([P, D_PM], BF16)
-        nc.gpsimd.dma_start(out=bias_bf[:], in_=proj_in_b.partition_broadcast(P))
-        gain_bf = const.tile([P, 1], BF16)
-        nc.gpsimd.dma_start(out=gain_bf[:], in_=surp_scale.partition_broadcast(P))
-        shift_bf = const.tile([P, 1], BF16)
-        nc.gpsimd.dma_start(out=shift_bf[:], in_=surp_bias.partition_broadcast(P))
-        gain = const.tile([P, 1], F32)
-        nc.gpsimd.tensor_copy(out=gain[:], in_=gain_bf[:])
-        shift = const.tile([P, 1], F32)
-        nc.gpsimd.tensor_copy(out=shift[:], in_=shift_bf[:])
+        small_rows = const.tile([P, D_PM + 2 * SMALL_STEP], BF16)
+        nc.vector.memset(small_rows[:], 0.0)
+        ones = const.tile([P, P], BF16)
+        nc.vector.memset(ones[:], 1.0)
+        nc.scalar.dma_start(out=small_rows[0:1, 0:D_PM], in_=proj_in_b.unsqueeze(0))
+        nc.scalar.dma_start(out=small_rows[0:1, D_PM : D_PM + 1], in_=surp_scale.unsqueeze(0))
+        nc.scalar.dma_start(out=small_rows[0:1, D_PM + SMALL_STEP : D_PM + SMALL_STEP + 1], in_=surp_bias.unsqueeze(0))
+        bias_psum = pre_psum.tile([P, D_PM], F32, name="acc")
+        nc.tensor.matmul(out=bias_psum[:], lhsT=ones[:], rhs=small_rows[:, 0:D_PM], start=True, stop=True)
+        bias_sb = const.tile([P, D_PM], F32)
+        nc.vector.tensor_copy(out=bias_sb[:], in_=bias_psum[:])
+        small_psum = pre_psum.tile([P, D_PM], F32, name="acc")
+        nc.tensor.matmul(
+            out=small_psum[:, 0 : 2 * SMALL_STEP], lhsT=ones[:], rhs=small_rows[:, D_PM:], start=True, stop=True
+        )
+        gain_shift = const.tile([P, 2 * SMALL_STEP], F32)
+        nc.vector.tensor_copy(out=gain_shift[:], in_=small_psum[:, 0 : 2 * SMALL_STEP])
+        gain = gain_shift[:, 0:1]
+        shift = gain_shift[:, SMALL_STEP : SMALL_STEP + 1]
 
         sum_sq = const.tile([P, CHUNKS, PACK], F32)
         mag = const.tile([P, CHUNKS, PACK], F32)
@@ -150,14 +160,14 @@ def tile_proceduralmemory_pa_kernel(
                 pre[c] = chunkwork.tile([P, PACK, D_PM], F32, name="pre")
             for j in range(HALF):
                 t = (u % HALVES) * HALF + j
-                nc.vector.tensor_tensor(out=pre[c][:, t, :], in0=acc[u, j][:], in1=bias_bf[:], op=ALU.add)
+                nc.vector.tensor_tensor(out=pre[c][:, t, :], in0=acc[u, j][:], in1=bias_sb[:], op=ALU.add)
 
         def magnitude(c):
             nc.gpsimd.tensor_tensor(out=mag[:, c, :], in0=sum_sq[:, c, :], in1=half_power[:], op=ALU.pow)
 
         def gate_of(c):
             nc.scalar.activation(
-                out=sig[:, c, :], in_=mag[:, c, :], func=ACT.Sigmoid, scale=gain[:, 0:1], bias=shift[:, 0:1]
+                out=sig[:, c, :], in_=mag[:, c, :], func=ACT.Sigmoid, scale=gain, bias=shift
             )
             nc.gpsimd.tensor_tensor(out=gate[:, c, :], in0=sig[:, c, :], in1=half_power[:], op=ALU.pow)
 

@@ -82,6 +82,12 @@ def tile_proceduralmemory_pa_kernel(
         wq_codes = const.tile([P, CHUNKS, D_PM], U32, align_bytes=64)
         wq_scales = const.tile([P, CHUNKS, D_PM], U8, align_bytes=64)
 
+        scale_rows = proj_in_w_scales.rearrange("g (q r) n -> q r g n", r=PACK)
+        for quadrant in range(PACK):
+            nc.sync.dma_start(
+                out=w_scales[32 * quadrant : 32 * quadrant + PACK, :, :].bitcast(I32),
+                in_=scale_rows[quadrant].bitcast(I32),
+            )
         s_sb, h_sb = [], []
         for u in range(UNITS):
             tiles = slice((u % HALVES) * HALF, (u % HALVES + 1) * HALF)
@@ -91,17 +97,11 @@ def tile_proceduralmemory_pa_kernel(
             h_half = inputs.tile([P, HALF, D], BF16, name="h_half")
             nc.sync.dma_start(out=h_half[:], in_=h_dram[u // HALVES][:, tiles, :])
             h_sb.append(h_half)
-            if u == 0:
+            if u == 1:
                 nc.sync.dma_start(
                     out=w_codes[:].bitcast(I32),
                     in_=proj_in_w_words.rearrange("g p n t -> p g (n t)").bitcast(I32),
                 )
-                scale_rows = proj_in_w_scales.rearrange("g (q r) n -> q r g n", r=PACK)
-                for quadrant in range(PACK):
-                    nc.sync.dma_start(
-                        out=w_scales[32 * quadrant : 32 * quadrant + PACK, :, :].bitcast(I32),
-                        in_=scale_rows[quadrant].bitcast(I32),
-                    )
 
         h_grouped, h_codes, h_scales, acc, pre, w_grouped, g_acc = {}, {}, {}, {}, {}, {}, {}
 
@@ -174,7 +174,14 @@ def tile_proceduralmemory_pa_kernel(
         def weigh(c):
             weighted = chunkwork.tile([P, PACK, D_PM], BF16, name="weighted")
             for t in range(PACK):
-                nc.vector.tensor_scalar_mul(out=weighted[:, t, :], in0=pre[c][:, t, :], scalar1=gate[:, c, t : t + 1])
+                if c == CHUNKS - 1:
+                    nc.scalar.activation(
+                        out=weighted[:, t, :], in_=pre[c][:, t, :], func=ACT.Copy, scale=gate[:, c, t : t + 1]
+                    )
+                else:
+                    nc.vector.tensor_scalar_mul(
+                        out=weighted[:, t, :], in0=pre[c][:, t, :], scalar1=gate[:, c, t : t + 1]
+                    )
             w_grouped[c] = chunkwork.tile([P, D_PM, PACK], BF16, align_bytes=64, name="w_grouped")
             nc.vector.tensor_copy(
                 out=w_grouped[c][:].rearrange("p (n i) t -> p n t i", i=4),

@@ -40,7 +40,7 @@ def tile_proceduralmemory_pa_kernel(
         name="outputs", bufs=M_TILES
     ) as outputs, tc.psum_pool(name="xt_psum", bufs=HALF) as xt_psum, tc.psum_pool(
         name="pre_psum", bufs=HALF
-    ) as pre_psum, tc.psum_pool(name="g_psum", bufs=M_TILES) as g_psum, tc.manual_schedule():
+    ) as pre_psum, tc.psum_pool(name="g_psum", bufs=M_TILES) as g_psum:
         w_scales = const.tile([P, K_GROUPS, D_PM], U8, align_bytes=64)
         nc.vector.memset(w_scales[:].bitcast(I32), 0)
         w_codes = const.tile([P, K_GROUPS, D_PM], U32, align_bytes=64)

@@ -22,6 +22,7 @@ HALVES = PACK // HALF
 M_TILES = D_PM // P
 UNITS = CHUNKS * HALVES
 SMALL_STEP = 16
+PSUM_BANKS = 8
 VECTOR_COPY_UNITS = 2
 
 FLOPS = 2 * SAMPLES * TOKENS * D * D_PM + 2 * SAMPLES * D_PM * D_PM * TOKENS
@@ -38,9 +39,7 @@ def tile_proceduralmemory_pa_kernel(
         name="work", bufs=3
     ) as work, tc.tile_pool(name="chunkwork", bufs=2) as chunkwork, tc.tile_pool(
         name="outputs", bufs=M_TILES
-    ) as outputs, tc.psum_pool(name="xt_psum", bufs=HALF) as xt_psum, tc.psum_pool(
-        name="pre_psum", bufs=HALF
-    ) as pre_psum, tc.psum_pool(name="g_psum", bufs=M_TILES) as g_psum:
+    ) as outputs, tc.psum_pool(name="banks", bufs=PSUM_BANKS) as banks:
         w_scales = const.tile([P, K_GROUPS, D_PM], U8, align_bytes=64)
         nc.vector.memset(w_scales[:].bitcast(I32), 0)
         w_codes = const.tile([P, K_GROUPS, D_PM], U32, align_bytes=64)
@@ -61,11 +60,11 @@ def tile_proceduralmemory_pa_kernel(
         nc.scalar.dma_start(out=small_rows[0:1, 0:D_PM], in_=proj_in_b.unsqueeze(0))
         nc.scalar.dma_start(out=small_rows[0:1, D_PM : D_PM + 1], in_=surp_scale.unsqueeze(0))
         nc.scalar.dma_start(out=small_rows[0:1, D_PM + SMALL_STEP : D_PM + SMALL_STEP + 1], in_=surp_bias.unsqueeze(0))
-        bias_psum = pre_psum.tile([P, D_PM], F32, name="acc")
+        bias_psum = banks.tile([P, D_PM], F32, name="bank")
         nc.tensor.matmul(out=bias_psum[:], lhsT=ones[:], rhs=small_rows[:, 0:D_PM], start=True, stop=True)
         bias_sb = const.tile([P, D_PM], F32)
         nc.vector.tensor_copy(out=bias_sb[:], in_=bias_psum[:])
-        small_psum = pre_psum.tile([P, D_PM], F32, name="acc")
+        small_psum = banks.tile([P, D_PM], F32, name="bank")
         nc.tensor.matmul(
             out=small_psum[:, 0 : 2 * SMALL_STEP], lhsT=ones[:], rhs=small_rows[:, D_PM:], start=True, stop=True
         )
@@ -118,7 +117,7 @@ def tile_proceduralmemory_pa_kernel(
             h_grouped[u] = work.tile([P, HALF, K_GROUPS * P * PACK], BF16, align_bytes=64, name="h_grouped")
             for j in range(HALF):
                 h_words = h_sb[u][:, j, :].bitcast(F32)
-                xt = xt_psum.tile([P, K_GROUPS, 2, P], F32, name="xt")
+                xt = banks.tile([P, K_GROUPS, 2, P], F32, name="bank")
                 for g in range(K_GROUPS):
                     for w in range(2):
                         first = g * (K_PASS // 2) + w
@@ -142,7 +141,7 @@ def tile_proceduralmemory_pa_kernel(
 
         def project(u):
             for j in range(HALF):
-                acc[u, j] = pre_psum.tile([P, D_PM], F32, name="acc")
+                acc[u, j] = banks.tile([P, D_PM], F32, name="bank")
                 for g in range(K_GROUPS):
                     nc.tensor.matmul_mx(
                         out=acc[u, j][:],
@@ -200,7 +199,7 @@ def tile_proceduralmemory_pa_kernel(
             for m in range(M_TILES):
                 rows = slice(m * P, (m + 1) * P)
                 if q == 0:
-                    g_acc[b, m] = g_psum.tile([P, D_PM], F32, name="g_acc")
+                    g_acc[b, m] = banks.tile([P, D_PM], F32, name="bank")
                 nc.tensor.matmul_mx(
                     out=g_acc[b, m][:],
                     lhsT=wq_codes[:, c, rows].bitcast(FP8X4),

@@ -90,12 +90,24 @@ def tile_proceduralmemory_pa_kernel(
         s_sb, h_sb = [], []
         for u in range(UNITS):
             tiles = slice((u % HALVES) * HALF, (u % HALVES + 1) * HALF)
+            if u == 0:
+                s_first, h_first = [], []
+                for j in range(HALF):
+                    s_one = inputs.tile([P, D], BF16, name="s_one")
+                    nc.sync.dma_start(out=s_one[:], in_=s_dram[0][:, j, :])
+                    s_first.append(s_one[:])
+                    h_one = inputs.tile([P, D], BF16, name="h_one")
+                    nc.sync.dma_start(out=h_one[:], in_=h_dram[0][:, j, :])
+                    h_first.append(h_one[:])
+                s_sb.append(s_first)
+                h_sb.append(h_first)
+                continue
             s_half = inputs.tile([P, HALF, D], BF16, name="s_half")
             nc.sync.dma_start(out=s_half[:], in_=s_dram[u // HALVES][:, tiles, :])
-            s_sb.append(s_half)
+            s_sb.append([s_half[:, j, :] for j in range(HALF)])
             h_half = inputs.tile([P, HALF, D], BF16, name="h_half")
             nc.sync.dma_start(out=h_half[:], in_=h_dram[u // HALVES][:, tiles, :])
-            h_sb.append(h_half)
+            h_sb.append([h_half[:, j, :] for j in range(HALF)])
             if u == 1:
                 nc.sync.dma_start(
                     out=w_codes[:].bitcast(I32),
@@ -109,14 +121,14 @@ def tile_proceduralmemory_pa_kernel(
                 t = (u % HALVES) * HALF + j
                 squares = work.tile([P, D], BF16, name="squares")
                 nc.scalar.activation(
-                    out=squares[:], in_=s_sb[u][:, j, :], func=ACT.Square,
+                    out=squares[:], in_=s_sb[u][j], func=ACT.Square,
                     accum_out=sum_sq[:, u // HALVES, t : t + 1],
                 )
 
         def transpose_h(u):
             h_grouped[u] = work.tile([P, HALF, K_GROUPS * P * PACK], BF16, align_bytes=64, name="h_grouped")
             for j in range(HALF):
-                h_words = h_sb[u][:, j, :].bitcast(F32)
+                h_words = h_sb[u][j].bitcast(F32)
                 xt = banks.tile([P, K_GROUPS, 2, P], F32, name="bank")
                 for g in range(K_GROUPS):
                     for w in range(2):

@@ -142,6 +142,19 @@ def tile_proceduralmemory_pa_kernel(
                 else:
                     nc.scalar.copy(out=grouped_words, in_=xt[:].rearrange("p g w n -> p g n w"))
 
+        def keep_clock(u):
+            spare = banks.tile([P, D_PM], F32, name="bank")
+            for j in range(HALF):
+                nc.tensor.matmul_mx(
+                    out=spare[:],
+                    lhsT=h_codes[u][:, j, 0, :].bitcast(FP8X4),
+                    lhsT_scale=h_scales[u][:, j, 0, :],
+                    rhs=w_codes[:, 0, :].bitcast(FP8X4),
+                    rhs_scale=w_scales[:, 0, :],
+                    start=True,
+                    stop=True,
+                )
+
         def quantise_h(u):
             h_codes[u] = work.tile([P, HALF, K_GROUPS, P], U32, align_bytes=64, name="h_codes")
             h_scales[u] = work.tile([P, HALF, K_GROUPS, P], U8, align_bytes=64, name="h_scales")
@@ -244,6 +257,8 @@ def tile_proceduralmemory_pa_kernel(
                 quantise_h(s - 1)
             if s < UNITS:
                 transpose_h(s)
+            if 2 <= s < UNITS:
+                keep_clock(s - 2)
             if 0 <= s - 1 < UNITS:
                 project(s - 1)
             if s >= 4 and s % HALVES == 0:

@@ -155,6 +155,10 @@ def tile_proceduralmemory_pa_kernel(
                     stop=True,
                 )
 
+        def spare_plain(moving):
+            spare = banks.tile([P, D_PM], F32, name="bank")
+            nc.tensor.matmul(out=spare[:], lhsT=ones[:], rhs=moving, start=True, stop=True)
+
         def quantise_h(u):
             h_codes[u] = work.tile([P, HALF, K_GROUPS, P], U32, align_bytes=64, name="h_codes")
             h_scales[u] = work.tile([P, HALF, K_GROUPS, P], U8, align_bytes=64, name="h_scales")
@@ -185,6 +189,16 @@ def tile_proceduralmemory_pa_kernel(
             for j in range(HALF):
                 t = (u % HALVES) * HALF + j
                 nc.vector.tensor_tensor(out=pre[c][:, t, :], in0=acc[u, j][:], in1=bias_sb[:], op=ALU.add)
+                if u == UNITS - 1:
+                    nc.tensor.matmul_mx(
+                        out=acc[u, j][:],
+                        lhsT=h_codes[u][:, j, 0, :].bitcast(FP8X4),
+                        lhsT_scale=h_scales[u][:, j, 0, :],
+                        rhs=w_codes[:, 0, :].bitcast(FP8X4),
+                        rhs_scale=w_scales[:, 0, :],
+                        start=True,
+                        stop=True,
+                    )
 
         def magnitude(c):
             nc.gpsimd.tensor_tensor(out=mag[:, c, :], in0=sum_sq[:, c, :], in1=half_power[:], op=ALU.pow)
@@ -211,6 +225,12 @@ def tile_proceduralmemory_pa_kernel(
                 out=w_grouped[c][:].rearrange("p (n i) t -> p n t i", i=4),
                 in_=weighted[:].rearrange("p t (n i) -> p n t i", i=4),
             )
+            if c == CHUNKS - 1:
+                for t in (PACK - 2, PACK - 1):
+                    spare_plain(weighted[:, t, :])
+                flat = w_grouped[c][:].rearrange("p n t -> p (n t)")
+                for half in range(HALF):
+                    spare_plain(flat[:, half * D_PM : (half + 1) * D_PM])
 
         def quantise_weighted(c):
             nc.vector.quantize_mx(

import concourse.mybir as mybir
from concourse.masks import make_identity

F32 = mybir.dt.float32
BF16 = mybir.dt.bfloat16
I32 = mybir.dt.int32
U32 = mybir.dt.uint32
U8 = mybir.dt.uint8
FP8X4 = mybir.dt.float8_e4m3fn_x4
ALU = mybir.AluOpType
ACT = mybir.ActivationFunctionType

P = 128
PACK = 4
K_PASS = P * PACK
SAMPLES, TOKENS, D, D_PM = 2, 1024, 1024, 512
CHUNKS = SAMPLES * TOKENS // K_PASS
CHUNKS_PER_SAMPLE = TOKENS // K_PASS
K_GROUPS = D // K_PASS
HALF = 2
HALVES = PACK // HALF
M_TILES = D_PM // P
UNITS = CHUNKS * HALVES
SMALL_STEP = 16
PSUM_BANKS = 8
VECTOR_COPY_UNITS = 2

FLOPS = 2 * SAMPLES * TOKENS * D * D_PM + 2 * SAMPLES * D_PM * D_PM * TOKENS


def tile_proceduralmemory_pa_kernel(
    tc, H, surprise, proj_in_w_words, proj_in_w_scales, proj_in_b, surp_scale, surp_bias, out
):
    nc = tc.nc
    h_dram = H.flatten_outer_dims().rearrange("(c p t) k -> c p t k", p=P, t=PACK)
    s_dram = surprise.flatten_outer_dims().rearrange("(c p t) k -> c p t k", p=P, t=PACK)

    with tc.tile_pool(name="const", bufs=1) as const, tc.tile_pool(name="inputs", bufs=UNITS) as inputs, tc.tile_pool(
        name="work", bufs=3
    ) as work, tc.tile_pool(name="chunkwork", bufs=2) as chunkwork, tc.tile_pool(
        name="outputs", bufs=M_TILES
    ) as outputs, tc.psum_pool(name="banks", bufs=PSUM_BANKS) as banks:
        w_scales = const.tile([P, K_GROUPS, D_PM], U8, align_bytes=64)
        nc.vector.memset(w_scales[:].bitcast(I32), 0)
        w_codes = const.tile([P, K_GROUPS, D_PM], U32, align_bytes=64)

        one_column = const.tile([P, 1], F32)
        nc.vector.memset(one_column[:], 0.0)
        nc.scalar.activation(out=one_column[:], in_=one_column[:], func=ACT.Sigmoid)

        ident = const.tile([P, P], F32)
        make_identity(nc, ident[:])
        half_power = const.tile([P, PACK], F32)
        nc.gpsimd.memset(half_power[:], 0.5)

        small_rows = const.tile([P, D_PM + 2 * SMALL_STEP], BF16)
        nc.vector.memset(small_rows[:], 0.0)
        ones = const.tile([P, P], BF16)
        nc.vector.memset(ones[:], 1.0)
        nc.scalar.dma_start(out=small_rows[0:1, 0:D_PM], in_=proj_in_b.unsqueeze(0))
        nc.scalar.dma_start(out=small_rows[0:1, D_PM : D_PM + 1], in_=surp_scale.unsqueeze(0))
        nc.scalar.dma_start(out=small_rows[0:1, D_PM + SMALL_STEP : D_PM + SMALL_STEP + 1], in_=surp_bias.unsqueeze(0))
        bias_psum = banks.tile([P, D_PM], F32, name="bank")
        nc.tensor.matmul(out=bias_psum[:], lhsT=ones[:], rhs=small_rows[:, 0:D_PM], start=True, stop=True)
        bias_sb = const.tile([P, D_PM], F32)
        nc.vector.tensor_copy(out=bias_sb[:], in_=bias_psum[:])
        small_psum = banks.tile([P, D_PM], F32, name="bank")
        nc.tensor.matmul(
            out=small_psum[:, 0 : 2 * SMALL_STEP], lhsT=ones[:], rhs=small_rows[:, D_PM:], start=True, stop=True
        )
        gain_shift = const.tile([P, 2 * SMALL_STEP], F32)
        nc.vector.tensor_copy(out=gain_shift[:], in_=small_psum[:, 0 : 2 * SMALL_STEP])
        gain = gain_shift[:, 0:1]
        shift = gain_shift[:, SMALL_STEP : SMALL_STEP + 1]

        sum_sq = const.tile([P, CHUNKS, PACK], F32)
        mag = const.tile([P, CHUNKS, PACK], F32)
        sig = const.tile([P, CHUNKS, PACK], F32)
        gate = const.tile([P, CHUNKS, PACK], F32)

        wq_codes = const.tile([P, CHUNKS, D_PM], U32, align_bytes=64)
        wq_scales = const.tile([P, CHUNKS, D_PM], U8, align_bytes=64)

        scale_rows = proj_in_w_scales.rearrange("g (q r) n -> q r g n", r=PACK)
        for quadrant in range(PACK):
            nc.sync.dma_start(
                out=w_scales[32 * quadrant : 32 * quadrant + PACK, :, :].bitcast(I32),
                in_=scale_rows[quadrant].bitcast(I32),
            )
        s_sb, h_sb = [], []
        for u in range(UNITS):
            tiles = slice((u % HALVES) * HALF, (u % HALVES + 1) * HALF)
            if u == 0:
                s_first, h_first = [], []
                for j in range(HALF):
                    s_one = inputs.tile([P, D], BF16, name="s_one")
                    nc.sync.dma_start(out=s_one[:], in_=s_dram[0][:, j, :])
                    s_first.append(s_one[:])
                    h_one = inputs.tile([P, D], BF16, name="h_one")
                    nc.sync.dma_start(out=h_one[:], in_=h_dram[0][:, j, :])
                    h_first.append(h_one[:])
                s_sb.append(s_first)
                h_sb.append(h_first)
                continue
            s_half = inputs.tile([P, HALF, D], BF16, name="s_half")
            nc.sync.dma_start(out=s_half[:], in_=s_dram[u // HALVES][:, tiles, :])
            s_sb.append([s_half[:, j, :] for j in range(HALF)])
            h_half = inputs.tile([P, HALF, D], BF16, name="h_half")
            nc.sync.dma_start(out=h_half[:], in_=h_dram[u // HALVES][:, tiles, :])
            h_sb.append([h_half[:, j, :] for j in range(HALF)])
            if u == 1:
                nc.sync.dma_start(
                    out=w_codes[:].bitcast(I32),
                    in_=proj_in_w_words.rearrange("g p n t -> p g (n t)").bitcast(I32),
                )

        h_grouped, h_codes, h_scales, acc, pre, w_grouped, g_acc = {}, {}, {}, {}, {}, {}, {}

        def sums_of_squares(u):
            for j in range(HALF):
                t = (u % HALVES) * HALF + j
                squares = work.tile([P, D], BF16, name="squares")
                nc.scalar.activation(
                    out=squares[:], in_=s_sb[u][j], func=ACT.Square,
                    accum_out=sum_sq[:, u // HALVES, t : t + 1],
                )

        def transpose_h(u):
            h_grouped[u] = work.tile([P, HALF, K_GROUPS * P * PACK], BF16, align_bytes=64, name="h_grouped")
            for j in range(HALF):
                h_words = h_sb[u][j].bitcast(F32)
                xt = banks.tile([P, K_GROUPS, 2, P], F32, name="bank")
                for g in range(K_GROUPS):
                    for w in range(2):
                        first = g * (K_PASS // 2) + w
                        nc.tensor.transpose(
                            xt[:, g, w, :], h_words[:, first : (g + 1) * (K_PASS // 2) : 2], ident[:]
                        )
                grouped_words = h_grouped[u][:, j, :].bitcast(F32).rearrange("p (g n w) -> p g n w", g=K_GROUPS, w=2)
                if u < VECTOR_COPY_UNITS:
                    nc.vector.tensor_copy(out=grouped_words, in_=xt[:].rearrange("p g w n -> p g n w"))
                else:
                    nc.scalar.copy(out=grouped_words, in_=xt[:].rearrange("p g w n -> p g n w"))

        def keep_clock(u):
            spare = banks.tile([P, D_PM], F32, name="bank")
            for j in range(HALF):
                nc.tensor.matmul_mx(
                    out=spare[:],
                    lhsT=h_codes[u][:, j, 0, :].bitcast(FP8X4),
                    lhsT_scale=h_scales[u][:, j, 0, :],
                    rhs=w_codes[:, 0, :].bitcast(FP8X4),
                    rhs_scale=w_scales[:, 0, :],
                    start=True,
                    stop=True,
                )

        def spare_plain(moving):
            spare = banks.tile([P, D_PM], F32, name="bank")
            nc.tensor.matmul(out=spare[:], lhsT=ones[:], rhs=moving, start=True, stop=True)

        def quantise_h(u):
            h_codes[u] = work.tile([P, HALF, K_GROUPS, P], U32, align_bytes=64, name="h_codes")
            h_scales[u] = work.tile([P, HALF, K_GROUPS, P], U8, align_bytes=64, name="h_scales")
            nc.vector.quantize_mx(
                out=h_codes[u][:].rearrange("p j g n -> p (j g n)").bitcast(FP8X4),
                scales=h_scales[u][:].rearrange("p j g n -> p (j g n)"),
                in_=h_grouped[u][:].rearrange("p j x -> p (j x)"),
            )

        def project(u):
            for j in range(HALF):
                acc[u, j] = banks.tile([P, D_PM], F32, name="bank")
                for g in range(K_GROUPS):
                    nc.tensor.matmul_mx(
                        out=acc[u, j][:],
                        lhsT=h_codes[u][:, j, g, :].bitcast(FP8X4),
                        lhsT_scale=h_scales[u][:, j, g, :],
                        rhs=w_codes[:, g, :].bitcast(FP8X4),
                        rhs_scale=w_scales[:, g, :],
                        start=(g == 0),
                        stop=(g == K_GROUPS - 1),
                    )

        def add_bias(u):
            c = u // HALVES
            if u % HALVES == 0:
                pre[c] = chunkwork.tile([P, PACK, D_PM], F32, name="pre")
            for j in range(HALF):
                t = (u % HALVES) * HALF + j
                nc.vector.tensor_tensor(out=pre[c][:, t, :], in0=acc[u, j][:], in1=bias_sb[:], op=ALU.add)
                if u == UNITS - 1:
                    nc.tensor.matmul_mx(
                        out=acc[u, j][:],
                        lhsT=h_codes[u][:, j, 0, :].bitcast(FP8X4),
                        lhsT_scale=h_scales[u][:, j, 0, :],
                        rhs=w_codes[:, 0, :].bitcast(FP8X4),
                        rhs_scale=w_scales[:, 0, :],
                        start=True,
                        stop=True,
                    )

        def magnitude(c):
            nc.gpsimd.tensor_tensor(out=mag[:, c, :], in0=sum_sq[:, c, :], in1=half_power[:], op=ALU.pow)

        def gate_of(c):
            nc.scalar.activation(
                out=sig[:, c, :], in_=mag[:, c, :], func=ACT.Sigmoid, scale=gain, bias=shift
            )
            nc.gpsimd.tensor_tensor(out=gate[:, c, :], in0=sig[:, c, :], in1=half_power[:], op=ALU.pow)

        def weigh(c):
            weighted = chunkwork.tile([P, PACK, D_PM], BF16, name="weighted")
            for t in range(PACK):
                if c == CHUNKS - 1:
                    nc.scalar.activation(
                        out=weighted[:, t, :], in_=pre[c][:, t, :], func=ACT.Copy, scale=gate[:, c, t : t + 1]
                    )
                else:
                    nc.vector.tensor_scalar_mul(
                        out=weighted[:, t, :], in0=pre[c][:, t, :], scalar1=gate[:, c, t : t + 1]
                    )
            w_grouped[c] = chunkwork.tile([P, D_PM, PACK], BF16, align_bytes=64, name="w_grouped")
            nc.vector.tensor_copy(
                out=w_grouped[c][:].rearrange("p (n i) t -> p n t i", i=4),
                in_=weighted[:].rearrange("p t (n i) -> p n t i", i=4),
            )
            if c == CHUNKS - 1:
                for t in (PACK - 2, PACK - 1):
                    spare_plain(weighted[:, t, :])
                flat = w_grouped[c][:].rearrange("p n t -> p (n t)")
                for half in range(HALF):
                    spare_plain(flat[:, half * D_PM : (half + 1) * D_PM])

        def quantise_weighted(c):
            nc.vector.quantize_mx(
                out=wq_codes[:, c, :].bitcast(FP8X4),
                scales=wq_scales[:, c, :],
                in_=w_grouped[c][:].rearrange("p n t -> p (n t)"),
            )

        def gram_pass(c):
            b, q = c // CHUNKS_PER_SAMPLE, c % CHUNKS_PER_SAMPLE
            for m in range(M_TILES):
                rows = slice(m * P, (m + 1) * P)
                if q == 0:
                    g_acc[b, m] = banks.tile([P, D_PM], F32, name="bank")
                nc.tensor.matmul_mx(
                    out=g_acc[b, m][:],
                    lhsT=wq_codes[:, c, rows].bitcast(FP8X4),
                    lhsT_scale=wq_scales[:, c, rows],
                    rhs=wq_codes[:, c, :].bitcast(FP8X4),
                    rhs_scale=wq_scales[:, c, :],
                    start=(q == 0),
                    stop=(q == CHUNKS_PER_SAMPLE - 1),
                )

        def store_gram(b):
            for m in range(M_TILES):
                g_sb = outputs.tile([P, D_PM], F32, name="g_sb")
                if b == SAMPLES - 1 and m % 2 == 1:
                    nc.vector.tensor_scalar_mul(out=g_sb[:], in0=g_acc[b, m][:], scalar1=1.0 / TOKENS)
                else:
                    nc.scalar.mul(out=g_sb[:], in_=g_acc[b, m][:], mul=1.0 / TOKENS)
                nc.sync.dma_start(out=out[b, m * P : (m + 1) * P, :], in_=g_sb[:])

        for s in range(UNITS + 3):
            if s < UNITS:
                sums_of_squares(s)
                if s % HALVES == HALVES - 1:
                    magnitude(s // HALVES)
            if HALVES <= s <= UNITS and s % HALVES == 0:
                gate_of(s // HALVES - 1)
            if s == UNITS:
                store_gram(0)
            if 0 <= s - 1 < UNITS:
                quantise_h(s - 1)
            if s < UNITS:
                transpose_h(s)
            if 2 <= s < UNITS:
                keep_clock(s - 2)
            if 0 <= s - 1 < UNITS:
                project(s - 1)
            if s >= 4 and s % HALVES == 0:
                quantise_weighted((s - 4) // HALVES)
                gram_pass((s - 4) // HALVES)
            if 0 <= s - 2 < UNITS:
                add_bias(s - 2)
            if s >= 3 and s % HALVES == 1:
                weigh((s - 3) // HALVES)
        store_gram(1)
